import numpy as np
import ml_dtypes


def mxq(x, axis, fmt="e4m3"):
    dtype, down = {"e4m3": (ml_dtypes.float8_e4m3fn, 7), "e5m2": (ml_dtypes.float8_e5m2, 14)}[fmt]
    v = np.moveaxis(np.asarray(x, np.float32).astype(ml_dtypes.bfloat16).astype(np.float64), axis, -1)
    blocks = v.reshape(v.shape[:-1] + (-1, 32))
    amax = np.abs(blocks).max(-1, keepdims=True)
    byte = np.maximum(np.where(amax > 0, np.frexp(amax)[1] - 1 + 127, 0) - down, 1)
    scale = np.exp2(byte - 127.0)
    codes = (blocks / scale).astype(np.float32).astype(dtype).astype(np.float64)
    return np.moveaxis((codes * scale).reshape(v.shape), -1, axis)


WIDE = False


def mx_kscale(k):
    if not WIDE:
        return np.ones(k)
    levels = np.array([20, -20, 10, -10, 0])
    a = np.random.permutation(np.resize(levels, k // 512 * 4)).reshape(k // 512, 4)
    idx = np.arange(k)
    return np.exp2(a[idx // 512, idx % 128 // 32])


BF16 = ml_dtypes.bfloat16


def bf(x):
    return np.asarray(x, np.float32).astype(BF16)


def f64(x):
    return np.asarray(x).astype(np.float64)


B, IN, H, Z, G = 512, 1024, 1024, 256, 4


def gate_scales(zx, dx_w):
    return (f64(zx).transpose(1, 0, 2) @ f64(dx_w).transpose(0, 2, 1)).transpose(1, 0, 2)


def setup_inputs():
    u = mx_kscale(G * H).reshape(G, H)
    src_x = bf(np.random.standard_normal((B, IN)))
    zx = bf(np.random.standard_normal((B, G, Z)))
    dx_w = bf(np.random.standard_normal((G, H, Z)) / np.sqrt(Z))
    w_x = bf(np.random.standard_normal((G, H, IN)) / np.sqrt(IN) / u[:, :, None])
    g = bf(np.random.standard_normal((B, G, H)) * np.exp2(np.random.randint(-12, 1, (B, 1, 1))) * 8.0 * u[None, :, :])
    d_x = gate_scales(zx, dx_w)
    return {"src_x": src_x, "zx": zx, "dx_w": dx_w, "w_x": w_x,
            "d_x": np.asarray(d_x, np.float32), "grad_out": g}


def reference(src_x, zx, dx_w, w_x, d_x, grad_out):
    dwx = (f64(grad_out) * f64(d_x)).reshape(B, G * H)
    return mxq(dwx, 1, "e5m2") @ mxq(f64(w_x).reshape(G * H, IN), 0, "e4m3")

@@ -1,0 +1,186 @@
+from contextlib import ExitStack
+
+import concourse.mybir as mybir
+from concourse.masks import make_identity
+
+BF16 = mybir.dt.bfloat16
+F32 = mybir.dt.float32
+U32 = mybir.dt.uint32
+U8 = mybir.dt.uint8
+E4M3_X4 = mybir.dt.float8_e4m3fn_x4
+E5M2_X4 = mybir.dt.float8_e5m2_x4
+
+B, IN, H, G = 512, 1024, 1024, 4
+K = G * H
+
+P = 128
+PACK = 4
+K_PASS = P * PACK
+PASSES = K // K_PASS
+GATE_PASSES = H // K_PASS
+N_HALF = 512
+HALVES = IN // N_HALF
+B_TILES = B // P
+LEAD = 3
+W_RAW_BUFS = 5
+
+FLOPS = 2 * B * K * IN
+BYTES = 2 * K * IN + 4 * B * K + 2 * B * K + 4 * B * IN
+
+
+def tile_metalstmcell_pa_v_kernel(tc, src_x, zx, dx_w, w_x, d_x, grad_out, out):
+    nc = tc.nc
+    w_rows = w_x.rearrange("g h i -> (g h) i")
+
+    with ExitStack() as ctx:
+        const = ctx.enter_context(tc.tile_pool(name="const", bufs=1))
+        keep = ctx.enter_context(tc.tile_pool(name="keep", bufs=1))
+        w_raw_pool = ctx.enter_context(tc.tile_pool(name="w_raw", bufs=W_RAW_BUFS))
+        w_grp_pool = ctx.enter_context(tc.tile_pool(name="w_grp", bufs=3))
+        g_pool = ctx.enter_context(tc.tile_pool(name="g_in", bufs=LEAD))
+        d_pool = ctx.enter_context(tc.tile_pool(name="d_in", bufs=LEAD * G))
+        x_work = ctx.enter_context(tc.tile_pool(name="x_work", bufs=2))
+        x_keep = ctx.enter_context(tc.tile_pool(name="x_keep", bufs=B_TILES))
+        out_pool = ctx.enter_context(tc.tile_pool(name="out_sb", bufs=B_TILES * HALVES))
+        acc_pool = ctx.enter_context(tc.psum_pool(name="acc", bufs=LEAD))
+        xt_pool = ctx.enter_context(tc.psum_pool(name="xt", bufs=8 - HALVES * LEAD))
+        ctx.enter_context(tc.manual_schedule())
+
+        ident = const.tile([P, P], F32)
+        make_identity(nc, ident[:])
+
+        w_codes = keep.tile([P, PASSES, IN], U32, align_bytes=64)
+        w_scales = keep.tile([P, PASSES, IN], U8, align_bytes=64)
+
+        w_raw = {}
+        w_grp = {}
+        g_in = {}
+        d_in = {}
+        x_grp = {}
+        x_codes = {}
+        x_scales = {}
+        acc = {}
+
+        def load_w(c):
+            w_raw[c] = w_raw_pool.tile([P, PACK, IN], BF16, name="w_raw")
+            nc.sync.dma_start(
+                out=w_raw[c][:],
+                in_=w_rows[c * K_PASS : (c + 1) * K_PASS, :].rearrange("(p j) i -> p j i", j=PACK),
+            )
+
+        def regroup_w(c):
+            w_grp[c] = w_grp_pool.tile([P, IN, PACK], BF16, name="w_grp", align_bytes=64)
+            for half, copy in ((0, nc.vector.tensor_copy), (1, nc.scalar.copy)):
+                cols = slice(half * N_HALF, (half + 1) * N_HALF)
+                copy(
+                    out=w_grp[c][:, cols, :].rearrange("p (n i) j -> p n j i", i=4),
+                    in_=w_raw[c][:, :, cols].rearrange("p j (n i) -> p n j i", i=4),
+                )
+
+        def quantise_w(c):
+            nc.vector.quantize_mx(
+                out=w_codes[:, c, :].bitcast(E4M3_X4),
+                scales=w_scales[:, c, :],
+                in_=w_grp[c][:].rearrange("p n j -> p (n j)"),
+            )
+
+        def load_x(bt):
+            rows = slice(bt * P, (bt + 1) * P)
+            g_in[bt] = g_pool.tile([P, K], BF16, name="g_in")
+            nc.sync.dma_start(out=g_in[bt][:], in_=grad_out[rows].rearrange("b g h -> b (g h)"))
+            for gate in range(G):
+                d_in[bt, gate] = d_pool.tile([P, H], F32, name="d_in")
+                nc.sync.dma_start(out=d_in[bt, gate][:], in_=d_x[rows, gate, :])
+            x_codes[bt] = x_keep.tile([P, PASSES, P], U32, name="x_codes", align_bytes=64)
+            x_scales[bt] = x_keep.tile([P, PASSES, P], U8, name="x_scales", align_bytes=64)
+
+        def turn_x(bt, gate):
+            dwx = x_work.tile([P, H], BF16, name="dwx")
+            nc.vector.tensor_tensor(
+                out=dwx[:].rearrange("p (u q e) -> p q u e", u=2, e=2),
+                in0=g_in[bt][:, gate * H : (gate + 1) * H].rearrange("p (q u e) -> p q u e", u=2, e=2),
+                in1=d_in[bt, gate][:].rearrange("p (q u e) -> p q u e", u=2, e=2),
+                op=mybir.AluOpType.mult,
+            )
+            dwx_words = dwx[:].bitcast(F32)
+            xt = xt_pool.tile([P, GATE_PASSES * 2 * P], F32, name="xt")
+            for c in range(GATE_PASSES):
+                for u in range(2):
+                    nc.tensor.transpose(
+                        xt[:, (c * 2 + u) * P : (c * 2 + u + 1) * P],
+                        dwx_words[:, (u * GATE_PASSES + c) * P : (u * GATE_PASSES + c + 1) * P],
+                        ident[:],
+                    )
+            x_grp[bt, gate] = x_work.tile([P, GATE_PASSES * P * PACK], BF16, name="x_grp", align_bytes=64)
+            nc.scalar.copy(
+                out=x_grp[bt, gate][:].bitcast(F32).rearrange("p (c b u) -> p c b u", c=GATE_PASSES, u=2),
+                in_=xt[:].rearrange("p (c u b) -> p c b u", c=GATE_PASSES, u=2),
+            )
+
+        def quantise_x(bt, gate):
+            passes = slice(gate * GATE_PASSES, (gate + 1) * GATE_PASSES)
+            nc.vector.quantize_mx(
+                out=x_codes[bt][:, passes, :].rearrange("p c b -> p (c b)").bitcast(E5M2_X4),
+                scales=x_scales[bt][:, passes, :].rearrange("p c b -> p (c b)"),
+                in_=x_grp[bt, gate][:],
+            )
+
+        def multiply(bt, c):
+            for half in range(HALVES):
+                if c == 0:
+                    acc[bt, half] = acc_pool.tile([P, N_HALF], F32, name="acc%d" % half)
+                cols = slice(half * N_HALF, (half + 1) * N_HALF)
+                nc.tensor.matmul_mx(
+                    out=acc[bt, half][:],
+                    lhsT=x_codes[bt][:, c, :].bitcast(E5M2_X4),
+                    lhsT_scale=x_scales[bt][:, c, :],
+                    rhs=w_codes[:, c, cols].bitcast(E4M3_X4),
+                    rhs_scale=w_scales[:, c, cols],
+                    start=(c == 0),
+                    stop=(c == PASSES - 1),
+                )
+
+        def store(bt):
+            for half in range(HALVES):
+                out_sb = out_pool.tile([P, N_HALF], F32, name="out_sb")
+                nc.scalar.copy(out=out_sb[:], in_=acc[bt, half][:])
+                nc.sync.dma_start(
+                    out=out[bt * P : (bt + 1) * P, half * N_HALF : (half + 1) * N_HALF], in_=out_sb[:]
+                )
+
+        for bt in range(LEAD):
+            load_x(bt)
+        for c in range(W_RAW_BUFS):
+            load_w(c)
+
+        lead_pieces = [(bt, gate) for bt in range(LEAD) for gate in range(G)]
+        for n, piece in enumerate(lead_pieces):
+            turn_x(*piece)
+            if n > 0:
+                quantise_x(*lead_pieces[n - 1])
+        quantise_x(*lead_pieces[-1])
+
+        regroup_w(0)
+        for c in range(PASSES):
+            if c + W_RAW_BUFS < PASSES:
+                load_w(c + W_RAW_BUFS)
+            if c + 1 < PASSES:
+                regroup_w(c + 1)
+            quantise_w(c)
+            for bt in range(LEAD):
+                multiply(bt, c)
+
+        last = B_TILES - 1
+        load_x(last)
+        for gate in range(G):
+            if gate < LEAD:
+                store(gate)
+            turn_x(last, gate)
+            if gate > 0:
+                quantise_x(last, gate - 1)
+                for c in range(GATE_PASSES):
+                    multiply(last, (gate - 1) * GATE_PASSES + c)
+        quantise_x(last, G - 1)
+        for c in range(GATE_PASSES):
+            multiply(last, (G - 1) * GATE_PASSES + c)
+        store(last)

@@ -22,7 +22,9 @@ N_HALF = 512
 HALVES = IN // N_HALF
 B_TILES = B // P
 LEAD = 3
-W_RAW_BUFS = 5
+PSUM_BANKS = 8
+LAG = 2
+AHEAD = 6
 
 FLOPS = 2 * B * K * IN
 BYTES = 2 * K * IN + 4 * B * K + 2 * B * K + 4 * B * IN
@@ -35,15 +37,14 @@ def tile_metalstmcell_pa_v_kernel(tc, src_x, zx, dx_w, w_x, d_x, grad_out, out):
     with ExitStack() as ctx:
         const = ctx.enter_context(tc.tile_pool(name="const", bufs=1))
         keep = ctx.enter_context(tc.tile_pool(name="keep", bufs=1))
-        w_raw_pool = ctx.enter_context(tc.tile_pool(name="w_raw", bufs=W_RAW_BUFS))
+        w_raw_pool = ctx.enter_context(tc.tile_pool(name="w_raw", bufs=4))
         w_grp_pool = ctx.enter_context(tc.tile_pool(name="w_grp", bufs=3))
-        g_pool = ctx.enter_context(tc.tile_pool(name="g_in", bufs=LEAD))
-        d_pool = ctx.enter_context(tc.tile_pool(name="d_in", bufs=LEAD * G))
-        x_work = ctx.enter_context(tc.tile_pool(name="x_work", bufs=2))
+        x_in_pool = ctx.enter_context(tc.tile_pool(name="x_in", bufs=8))
+        x_work = ctx.enter_context(tc.tile_pool(name="x_work", bufs=3))
         x_keep = ctx.enter_context(tc.tile_pool(name="x_keep", bufs=B_TILES))
         out_pool = ctx.enter_context(tc.tile_pool(name="out_sb", bufs=B_TILES * HALVES))
         acc_pool = ctx.enter_context(tc.psum_pool(name="acc", bufs=LEAD))
-        xt_pool = ctx.enter_context(tc.psum_pool(name="xt", bufs=8 - HALVES * LEAD))
+        xt_pool = ctx.enter_context(tc.psum_pool(name="xt", bufs=PSUM_BANKS - HALVES * LEAD))
         ctx.enter_context(tc.manual_schedule())
 
         ident = const.tile([P, P], F32)
@@ -84,21 +85,18 @@ def tile_metalstmcell_pa_v_kernel(tc, src_x, zx, dx_w, w_x, d_x, grad_out, out):
                 in_=w_grp[c][:].rearrange("p n j -> p (n j)"),
             )
 
-        def load_x(bt):
+        def load_x(bt, gate):
             rows = slice(bt * P, (bt + 1) * P)
-            g_in[bt] = g_pool.tile([P, K], BF16, name="g_in")
-            nc.sync.dma_start(out=g_in[bt][:], in_=grad_out[rows].rearrange("b g h -> b (g h)"))
-            for gate in range(G):
-                d_in[bt, gate] = d_pool.tile([P, H], F32, name="d_in")
-                nc.sync.dma_start(out=d_in[bt, gate][:], in_=d_x[rows, gate, :])
-            x_codes[bt] = x_keep.tile([P, PASSES, P], U32, name="x_codes", align_bytes=64)
-            x_scales[bt] = x_keep.tile([P, PASSES, P], U8, name="x_scales", align_bytes=64)
+            g_in[bt, gate] = x_in_pool.tile([P, H], BF16, name="g_in")
+            nc.sync.dma_start(out=g_in[bt, gate][:], in_=grad_out[rows, gate, :])
+            d_in[bt, gate] = x_in_pool.tile([P, H], F32, name="d_in")
+            nc.sync.dma_start(out=d_in[bt, gate][:], in_=d_x[rows, gate, :])
 
         def turn_x(bt, gate):
             dwx = x_work.tile([P, H], BF16, name="dwx")
             nc.vector.tensor_tensor(
                 out=dwx[:].rearrange("p (u q e) -> p q u e", u=2, e=2),
-                in0=g_in[bt][:, gate * H : (gate + 1) * H].rearrange("p (q u e) -> p q u e", u=2, e=2),
+                in0=g_in[bt, gate][:].rearrange("p (q u e) -> p q u e", u=2, e=2),
                 in1=d_in[bt, gate][:].rearrange("p (q u e) -> p q u e", u=2, e=2),
                 op=mybir.AluOpType.mult,
             )
@@ -118,6 +116,9 @@ def tile_metalstmcell_pa_v_kernel(tc, src_x, zx, dx_w, w_x, d_x, grad_out, out):
             )
 
         def quantise_x(bt, gate):
+            if gate == 0:
+                x_codes[bt] = x_keep.tile([P, PASSES, P], U32, name="x_codes", align_bytes=64)
+                x_scales[bt] = x_keep.tile([P, PASSES, P], U8, name="x_scales", align_bytes=64)
             passes = slice(gate * GATE_PASSES, (gate + 1) * GATE_PASSES)
             nc.vector.quantize_mx(
                 out=x_codes[bt][:, passes, :].rearrange("p c b -> p (c b)").bitcast(E5M2_X4),
@@ -125,20 +126,21 @@ def tile_metalstmcell_pa_v_kernel(tc, src_x, zx, dx_w, w_x, d_x, grad_out, out):
                 in_=x_grp[bt, gate][:],
             )
 
-        def multiply(bt, c):
-            for half in range(HALVES):
-                if c == 0:
-                    acc[bt, half] = acc_pool.tile([P, N_HALF], F32, name="acc%d" % half)
-                cols = slice(half * N_HALF, (half + 1) * N_HALF)
-                nc.tensor.matmul_mx(
-                    out=acc[bt, half][:],
-                    lhsT=x_codes[bt][:, c, :].bitcast(E5M2_X4),
-                    lhsT_scale=x_scales[bt][:, c, :],
-                    rhs=w_codes[:, c, cols].bitcast(E4M3_X4),
-                    rhs_scale=w_scales[:, c, cols],
-                    start=(c == 0),
-                    stop=(c == PASSES - 1),
-                )
+        def multiply(bt, gate):
+            for c in range(gate * GATE_PASSES, (gate + 1) * GATE_PASSES):
+                for half in range(HALVES):
+                    if c == 0:
+                        acc[bt, half] = acc_pool.tile([P, N_HALF], F32, name="acc%d" % half)
+                    cols = slice(half * N_HALF, (half + 1) * N_HALF)
+                    nc.tensor.matmul_mx(
+                        out=acc[bt, half][:],
+                        lhsT=x_codes[bt][:, c, :].bitcast(E5M2_X4),
+                        lhsT_scale=x_scales[bt][:, c, :],
+                        rhs=w_codes[:, c, cols].bitcast(E4M3_X4),
+                        rhs_scale=w_scales[:, c, cols],
+                        start=(c == 0),
+                        stop=(c == PASSES - 1),
+                    )
 
         def store(bt):
             for half in range(HALVES):
@@ -148,39 +150,43 @@ def tile_metalstmcell_pa_v_kernel(tc, src_x, zx, dx_w, w_x, d_x, grad_out, out):
                     out=out[bt * P : (bt + 1) * P, half * N_HALF : (half + 1) * N_HALF], in_=out_sb[:]
                 )
 
-        for bt in range(LEAD):
-            load_x(bt)
-        for c in range(W_RAW_BUFS):
-            load_w(c)
-
-        lead_pieces = [(bt, gate) for bt in range(LEAD) for gate in range(G)]
-        for n, piece in enumerate(lead_pieces):
-            turn_x(*piece)
-            if n > 0:
-                quantise_x(*lead_pieces[n - 1])
-        quantise_x(*lead_pieces[-1])
-
-        regroup_w(0)
-        for c in range(PASSES):
-            if c + W_RAW_BUFS < PASSES:
-                load_w(c + W_RAW_BUFS)
-            if c + 1 < PASSES:
-                regroup_w(c + 1)
-            quantise_w(c)
-            for bt in range(LEAD):
-                multiply(bt, c)
-
-        last = B_TILES - 1
-        load_x(last)
+        items = []
         for gate in range(G):
-            if gate < LEAD:
-                store(gate)
-            turn_x(last, gate)
-            if gate > 0:
-                quantise_x(last, gate - 1)
-                for c in range(GATE_PASSES):
-                    multiply(last, (gate - 1) * GATE_PASSES + c)
-        quantise_x(last, G - 1)
-        for c in range(GATE_PASSES):
-            multiply(last, (G - 1) * GATE_PASSES + c)
-        store(last)
+            for c in range(gate * GATE_PASSES, (gate + 1) * GATE_PASSES):
+                items.append(("weights", c))
+            for bt in range(LEAD):
+                items.append(("product", bt, gate))
+        for bt in range(LEAD, B_TILES):
+            for gate in range(G):
+                items.append(("product", bt, gate))
+
+        def load(item):
+            if item[0] == "weights":
+                load_w(item[1])
+            else:
+                load_x(item[1], item[2])
+
+        def first_half(item):
+            if item[0] == "weights":
+                regroup_w(item[1])
+            else:
+                turn_x(item[1], item[2])
+
+        def second_half(item):
+            if item[0] == "weights":
+                quantise_w(item[1])
+            else:
+                quantise_x(item[1], item[2])
+                multiply(item[1], item[2])
+                if item[2] == G - 1:
+                    store(item[1])
+
+        for n in range(AHEAD):
+            load(items[n])
+        for n in range(len(items) + LAG):
+            if n < len(items):
+                first_half(items[n])
+            if n + AHEAD < len(items):
+                load(items[n + AHEAD])
+            if n >= LAG:
+                second_half(items[n - LAG])

@@ -24,6 +24,7 @@ B_TILES = B // P
 LEAD = 3
 PSUM_BANKS = 8
 LAG = 2
+WARM = 3
 AHEAD = 6
 
 FLOPS = 2 * B * K * IN
@@ -49,6 +50,8 @@ def tile_metalstmcell_pa_v_kernel(tc, src_x, zx, dx_w, w_x, d_x, grad_out, out):
 
         ident = const.tile([P, P], F32)
         make_identity(nc, ident[:])
+        idle_rows = const.tile([P, N_HALF], BF16)
+        nc.vector.memset(idle_rows[:], 0.0)
 
         w_codes = keep.tile([P, PASSES, IN], U32, align_bytes=64)
         w_scales = keep.tile([P, PASSES, IN], U8, align_bytes=64)
@@ -114,6 +117,10 @@ def tile_metalstmcell_pa_v_kernel(tc, src_x, zx, dx_w, w_x, d_x, grad_out, out):
                 out=x_grp[bt, gate][:].bitcast(F32).rearrange("p (c b u) -> p c b u", c=GATE_PASSES, u=2),
                 in_=xt[:].rearrange("p (c u b) -> p c b u", c=GATE_PASSES, u=2),
             )
+            if gate == G - 1 and bt < LEAD:
+                idle_sums = xt_pool.tile([P, N_HALF], F32, name="xt")
+                for n in range(WARM):
+                    nc.tensor.matmul(idle_sums[:], lhsT=idle_rows[:, 0:P], rhs=idle_rows[:], start=True, stop=True)
 
         def quantise_x(bt, gate):
             if gate == 0:

@@ -117,7 +117,7 @@ def tile_metalstmcell_pa_v_kernel(tc, src_x, zx, dx_w, w_x, d_x, grad_out, out):
                 out=x_grp[bt, gate][:].bitcast(F32).rearrange("p (c b u) -> p c b u", c=GATE_PASSES, u=2),
                 in_=xt[:].rearrange("p (c u b) -> p c b u", c=GATE_PASSES, u=2),
             )
-            if gate == G - 1 and bt < LEAD:
+            if gate == G - 1 and bt < LEAD - 1:
                 idle_sums = xt_pool.tile([P, N_HALF], F32, name="xt")
                 for n in range(WARM):
                     nc.tensor.matmul(idle_sums[:], lhsT=idle_rows[:, 0:P], rhs=idle_rows[:], start=True, stop=True)

@@ -134,20 +134,24 @@ def tile_metalstmcell_pa_v_kernel(tc, src_x, zx, dx_w, w_x, d_x, grad_out, out):
             )
 
         def multiply(bt, gate):
-            for c in range(gate * GATE_PASSES, (gate + 1) * GATE_PASSES):
-                for half in range(HALVES):
-                    if c == 0:
-                        acc[bt, half] = acc_pool.tile([P, N_HALF], F32, name="acc%d" % half)
-                    cols = slice(half * N_HALF, (half + 1) * N_HALF)
-                    nc.tensor.matmul_mx(
-                        out=acc[bt, half][:],
-                        lhsT=x_codes[bt][:, c, :].bitcast(E5M2_X4),
-                        lhsT_scale=x_scales[bt][:, c, :],
-                        rhs=w_codes[:, c, cols].bitcast(E4M3_X4),
-                        rhs_scale=w_scales[:, c, cols],
-                        start=(c == 0),
-                        stop=(c == PASSES - 1),
-                    )
+            passes = range(gate * GATE_PASSES, (gate + 1) * GATE_PASSES)
+            if bt == B_TILES - 1 and gate == G - 1:
+                order = [(c, half) for half in range(HALVES) for c in passes]
+            else:
+                order = [(c, half) for c in passes for half in range(HALVES)]
+            for c, half in order:
+                if c == 0:
+                    acc[bt, half] = acc_pool.tile([P, N_HALF], F32, name="acc%d" % half)
+                cols = slice(half * N_HALF, (half + 1) * N_HALF)
+                nc.tensor.matmul_mx(
+                    out=acc[bt, half][:],
+                    lhsT=x_codes[bt][:, c, :].bitcast(E5M2_X4),
+                    lhsT_scale=x_scales[bt][:, c, :],
+                    rhs=w_codes[:, c, cols].bitcast(E4M3_X4),
+                    rhs_scale=w_scales[:, c, cols],
+                    start=(c == 0),
+                    stop=(c == PASSES - 1),
+                )
 
         def store(bt):
             for half in range(HALVES):
@@ -188,6 +192,11 @@ def tile_metalstmcell_pa_v_kernel(tc, src_x, zx, dx_w, w_x, d_x, grad_out, out):
                 if item[2] == G - 1:
                     store(item[1])
 
+        due = {}
+        for n in range(len(items)):
+            early = items[n][0] == "product" and items[n][2] == G - 1 and items[n][1] < LEAD - 1
+            due.setdefault(n + (LAG - 1 if early else LAG), []).append(items[n])
+
         for n in range(AHEAD):
             load(items[n])
         for n in range(len(items) + LAG):
@@ -195,5 +204,5 @@ def tile_metalstmcell_pa_v_kernel(tc, src_x, zx, dx_w, w_x, d_x, grad_out, out):
                 first_half(items[n])
             if n + AHEAD < len(items):
                 load(items[n + AHEAD])
-            if n >= LAG:
-                second_half(items[n - LAG])
+            for item in due.get(n, []):
+                second_half(item)

@@ -24,7 +24,6 @@ B_TILES = B // P
 LEAD = 3
 PSUM_BANKS = 8
 LAG = 2
-WARM = 3
 AHEAD = 6
 
 FLOPS = 2 * B * K * IN
@@ -50,8 +49,6 @@ def tile_metalstmcell_pa_v_kernel(tc, src_x, zx, dx_w, w_x, d_x, grad_out, out):
 
         ident = const.tile([P, P], F32)
         make_identity(nc, ident[:])
-        idle_rows = const.tile([P, N_HALF], BF16)
-        nc.vector.memset(idle_rows[:], 0.0)
 
         w_codes = keep.tile([P, PASSES, IN], U32, align_bytes=64)
         w_scales = keep.tile([P, PASSES, IN], U8, align_bytes=64)
@@ -117,10 +114,6 @@ def tile_metalstmcell_pa_v_kernel(tc, src_x, zx, dx_w, w_x, d_x, grad_out, out):
                 out=x_grp[bt, gate][:].bitcast(F32).rearrange("p (c b u) -> p c b u", c=GATE_PASSES, u=2),
                 in_=xt[:].rearrange("p (c u b) -> p c b u", c=GATE_PASSES, u=2),
             )
-            if gate == G - 1 and bt < LEAD - 1:
-                idle_sums = xt_pool.tile([P, N_HALF], F32, name="xt")
-                for n in range(WARM):
-                    nc.tensor.matmul(idle_sums[:], lhsT=idle_rows[:, 0:P], rhs=idle_rows[:], start=True, stop=True)
 
         def quantise_x(bt, gate):
             if gate == 0:
@@ -163,10 +156,16 @@ def tile_metalstmcell_pa_v_kernel(tc, src_x, zx, dx_w, w_x, d_x, grad_out, out):
 
         items = []
         for gate in range(G):
-            for c in range(gate * GATE_PASSES, (gate + 1) * GATE_PASSES):
-                items.append(("weights", c))
+            if gate < G - 1:
+                for c in range(gate * GATE_PASSES, (gate + 1) * GATE_PASSES):
+                    items.append(("weights", c))
             for bt in range(LEAD):
+                wrapped = gate == G - 2 and bt == LEAD - 1
+                if wrapped:
+                    items.append(("weights", PASSES - 2))
                 items.append(("product", bt, gate))
+                if wrapped:
+                    items.append(("weights", PASSES - 1))
         for bt in range(LEAD, B_TILES):
             for gate in range(G):
                 items.append(("product", bt, gate))

from contextlib import ExitStack

import concourse.mybir as mybir
from concourse.masks import make_identity

BF16 = mybir.dt.bfloat16
F32 = mybir.dt.float32
U32 = mybir.dt.uint32
U8 = mybir.dt.uint8
E4M3_X4 = mybir.dt.float8_e4m3fn_x4
E5M2_X4 = mybir.dt.float8_e5m2_x4

B, IN, H, G = 512, 1024, 1024, 4
K = G * H

P = 128
PACK = 4
K_PASS = P * PACK
PASSES = K // K_PASS
GATE_PASSES = H // K_PASS
N_HALF = 512
HALVES = IN // N_HALF
B_TILES = B // P
LEAD = 3
PSUM_BANKS = 8
LAG = 2
AHEAD = 6

FLOPS = 2 * B * K * IN
BYTES = 2 * K * IN + 4 * B * K + 2 * B * K + 4 * B * IN


def tile_metalstmcell_pa_v_kernel(tc, src_x, zx, dx_w, w_x, d_x, grad_out, out):
    nc = tc.nc
    w_rows = w_x.rearrange("g h i -> (g h) i")

    with ExitStack() as ctx:
        const = ctx.enter_context(tc.tile_pool(name="const", bufs=1))
        keep = ctx.enter_context(tc.tile_pool(name="keep", bufs=1))
        w_raw_pool = ctx.enter_context(tc.tile_pool(name="w_raw", bufs=4))
        w_grp_pool = ctx.enter_context(tc.tile_pool(name="w_grp", bufs=3))
        x_in_pool = ctx.enter_context(tc.tile_pool(name="x_in", bufs=8))
        x_work = ctx.enter_context(tc.tile_pool(name="x_work", bufs=3))
        x_keep = ctx.enter_context(tc.tile_pool(name="x_keep", bufs=B_TILES))
        out_pool = ctx.enter_context(tc.tile_pool(name="out_sb", bufs=B_TILES * HALVES))
        acc_pool = ctx.enter_context(tc.psum_pool(name="acc", bufs=LEAD))
        xt_pool = ctx.enter_context(tc.psum_pool(name="xt", bufs=PSUM_BANKS - HALVES * LEAD))
        ctx.enter_context(tc.manual_schedule())

        ident = const.tile([P, P], F32)
        make_identity(nc, ident[:])

        w_codes = keep.tile([P, PASSES, IN], U32, align_bytes=64)
        w_scales = keep.tile([P, PASSES, IN], U8, align_bytes=64)

        w_raw = {}
        w_grp = {}
        g_in = {}
        d_in = {}
        x_grp = {}
        x_codes = {}
        x_scales = {}
        acc = {}

        def load_w(c):
            w_raw[c] = w_raw_pool.tile([P, PACK, IN], BF16, name="w_raw")
            nc.sync.dma_start(
                out=w_raw[c][:],
                in_=w_rows[c * K_PASS : (c + 1) * K_PASS, :].rearrange("(p j) i -> p j i", j=PACK),
            )

        def regroup_w(c):
            w_grp[c] = w_grp_pool.tile([P, IN, PACK], BF16, name="w_grp", align_bytes=64)
            for half, copy in ((0, nc.vector.tensor_copy), (1, nc.scalar.copy)):
                cols = slice(half * N_HALF, (half + 1) * N_HALF)
                copy(
                    out=w_grp[c][:, cols, :].rearrange("p (n i) j -> p n j i", i=4),
                    in_=w_raw[c][:, :, cols].rearrange("p j (n i) -> p n j i", i=4),
                )

        def quantise_w(c):
            nc.vector.quantize_mx(
                out=w_codes[:, c, :].bitcast(E4M3_X4),
                scales=w_scales[:, c, :],
                in_=w_grp[c][:].rearrange("p n j -> p (n j)"),
            )

        def load_x(bt, gate):
            rows = slice(bt * P, (bt + 1) * P)
            g_in[bt, gate] = x_in_pool.tile([P, H], BF16, name="g_in")
            nc.sync.dma_start(out=g_in[bt, gate][:], in_=grad_out[rows, gate, :])
            d_in[bt, gate] = x_in_pool.tile([P, H], F32, name="d_in")
            nc.sync.dma_start(out=d_in[bt, gate][:], in_=d_x[rows, gate, :])

        def turn_x(bt, gate):
            dwx = x_work.tile([P, H], BF16, name="dwx")
            nc.vector.tensor_tensor(
                out=dwx[:].rearrange("p (u q e) -> p q u e", u=2, e=2),
                in0=g_in[bt, gate][:].rearrange("p (q u e) -> p q u e", u=2, e=2),
                in1=d_in[bt, gate][:].rearrange("p (q u e) -> p q u e", u=2, e=2),
                op=mybir.AluOpType.mult,
            )
            dwx_words = dwx[:].bitcast(F32)
            xt = xt_pool.tile([P, GATE_PASSES * 2 * P], F32, name="xt")
            for c in range(GATE_PASSES):
                for u in range(2):
                    nc.tensor.transpose(
                        xt[:, (c * 2 + u) * P : (c * 2 + u + 1) * P],
                        dwx_words[:, (u * GATE_PASSES + c) * P : (u * GATE_PASSES + c + 1) * P],
                        ident[:],
                    )
            x_grp[bt, gate] = x_work.tile([P, GATE_PASSES * P * PACK], BF16, name="x_grp", align_bytes=64)
            nc.scalar.copy(
                out=x_grp[bt, gate][:].bitcast(F32).rearrange("p (c b u) -> p c b u", c=GATE_PASSES, u=2),
                in_=xt[:].rearrange("p (c u b) -> p c b u", c=GATE_PASSES, u=2),
            )

        def quantise_x(bt, gate):
            if gate == 0:
                x_codes[bt] = x_keep.tile([P, PASSES, P], U32, name="x_codes", align_bytes=64)
                x_scales[bt] = x_keep.tile([P, PASSES, P], U8, name="x_scales", align_bytes=64)
            passes = slice(gate * GATE_PASSES, (gate + 1) * GATE_PASSES)
            nc.vector.quantize_mx(
                out=x_codes[bt][:, passes, :].rearrange("p c b -> p (c b)").bitcast(E5M2_X4),
                scales=x_scales[bt][:, passes, :].rearrange("p c b -> p (c b)"),
                in_=x_grp[bt, gate][:],
            )

        def multiply(bt, gate):
            passes = range(gate * GATE_PASSES, (gate + 1) * GATE_PASSES)
            if bt == B_TILES - 1 and gate == G - 1:
                order = [(c, half) for half in range(HALVES) for c in passes]
            else:
                order = [(c, half) for c in passes for half in range(HALVES)]
            for c, half in order:
                if c == 0:
                    acc[bt, half] = acc_pool.tile([P, N_HALF], F32, name="acc%d" % half)
                cols = slice(half * N_HALF, (half + 1) * N_HALF)
                nc.tensor.matmul_mx(
                    out=acc[bt, half][:],
                    lhsT=x_codes[bt][:, c, :].bitcast(E5M2_X4),
                    lhsT_scale=x_scales[bt][:, c, :],
                    rhs=w_codes[:, c, cols].bitcast(E4M3_X4),
                    rhs_scale=w_scales[:, c, cols],
                    start=(c == 0),
                    stop=(c == PASSES - 1),
                )

        def store(bt):
            for half in range(HALVES):
                out_sb = out_pool.tile([P, N_HALF], F32, name="out_sb")
                nc.scalar.copy(out=out_sb[:], in_=acc[bt, half][:])
                nc.sync.dma_start(
                    out=out[bt * P : (bt + 1) * P, half * N_HALF : (half + 1) * N_HALF], in_=out_sb[:]
                )

        items = []
        for gate in range(G):
            if gate < G - 1:
                for c in range(gate * GATE_PASSES, (gate + 1) * GATE_PASSES):
                    items.append(("weights", c))
            for bt in range(LEAD):
                wrapped = gate == G - 2 and bt == LEAD - 1
                if wrapped:
                    items.append(("weights", PASSES - 2))
                items.append(("product", bt, gate))
                if wrapped:
                    items.append(("weights", PASSES - 1))
        for bt in range(LEAD, B_TILES):
            for gate in range(G):
                items.append(("product", bt, gate))

        def load(item):
            if item[0] == "weights":
                load_w(item[1])
            else:
                load_x(item[1], item[2])

        def first_half(item):
            if item[0] == "weights":
                regroup_w(item[1])
            else:
                turn_x(item[1], item[2])

        def second_half(item):
            if item[0] == "weights":
                quantise_w(item[1])
            else:
                quantise_x(item[1], item[2])
                multiply(item[1], item[2])
                if item[2] == G - 1:
                    store(item[1])

        due = {}
        for n in range(len(items)):
            early = items[n][0] == "product" and items[n][2] == G - 1 and items[n][1] < LEAD - 1
            due.setdefault(n + (LAG - 1 if early else LAG), []).append(items[n])

        for n in range(AHEAD):
            load(items[n])
        for n in range(len(items) + LAG):
            if n < len(items):
                first_half(items[n])
            if n + AHEAD < len(items):
                load(items[n + AHEAD])
            for item in due.get(n, []):
                second_half(item)
